import numpy as np
import ml_dtypes


def mxq(x, axis, fmt="e4m3"):
    dtype, down = {"e4m3": (ml_dtypes.float8_e4m3fn, 7), "e5m2": (ml_dtypes.float8_e5m2, 14)}[fmt]
    v = np.moveaxis(np.asarray(x, np.float32).astype(ml_dtypes.bfloat16).astype(np.float64), axis, -1)
    blocks = v.reshape(v.shape[:-1] + (-1, 32))
    amax = np.abs(blocks).max(-1, keepdims=True)
    byte = np.maximum(np.where(amax > 0, np.frexp(amax)[1] - 1 + 127, 0) - down, 1)
    scale = np.exp2(byte - 127.0)
    codes = (blocks / scale).astype(np.float32).astype(dtype).astype(np.float64)
    return np.moveaxis((codes * scale).reshape(v.shape), -1, axis)


WIDE = False


def mx_kscale(k):
    if not WIDE:
        return np.ones(k)
    levels = np.array([10, -10, 5, -5, 0])
    if k % 512:
        return np.exp2(np.random.permutation(np.resize(levels, k // 32))).repeat(32)
    a = np.empty((k // 512, 16))
    for p in range(k // 512):
        a[p, :8] = np.random.permutation(np.resize(levels, 8))
        for g in range(8):
            far = levels[np.abs(levels - a[p, g]) >= 10]
            a[p, g + 8] = far[np.random.randint(len(far))]
    return np.exp2(a.ravel()).repeat(32)


BF16 = ml_dtypes.bfloat16


def bf(x):
    return np.asarray(x, np.float32).astype(BF16)


def f64(x):
    return np.asarray(x).astype(np.float64)


B, N, D, R = 8, 1024, 512, 4
M = N // R


def merge(t, r):
    b, n, d = t.shape
    return t.reshape(b, n // r, r, d).mean(axis=2)


def setup_inputs():
    s, t = mx_kscale(D), mx_kscale(D)
    a = 2.0 / np.sqrt(D)
    return {"x": bf(np.random.standard_normal((B, N, D)) * s),
            "Wq": bf(np.random.standard_normal((D, D)) * a * t[:, None] / s),
            "bq": bf(np.random.standard_normal(D) * 0.5 * t),
            "Wk": bf(np.random.standard_normal((D, D)) * a / t[:, None] / s),
            "bk": bf(np.random.standard_normal(D) * 0.3 / t)}


def reference(x, Wq, bq, Wk, bk):
    xq = mxq(f64(x), 2, "e4m3")
    Q = (xq @ mxq(f64(Wq), 1, "e4m3").T) + f64(bq)
    K = (xq @ mxq(f64(Wk), 1, "e4m3").T) + f64(bk)
    K_m = merge(K, R)
    scores = (mxq(Q, 2, "e4m3") @ mxq(K_m, 2, "e4m3").transpose(0, 2, 1)) * (1.0 / np.sqrt(D))
    return scores + np.log(R)

@@ -1,0 +1,223 @@
+import math
+from contextlib import ExitStack
+
+import concourse.mybir as mybir
+from concourse.masks import make_identity
+
+F32 = mybir.dt.float32
+BF16 = mybir.dt.bfloat16
+U32 = mybir.dt.uint32
+U8 = mybir.dt.uint8
+FP8X4 = mybir.dt.float8_e4m3fn_x4
+ADD = mybir.AluOpType.add
+MULT = mybir.AluOpType.mult
+IDENTITY = mybir.ActivationFunctionType.Identity
+COPY = mybir.ActivationFunctionType.Copy
+
+P = 128
+PACK = 4
+D = P * PACK
+BATCH = 8
+TOKENS = 1024
+WINDOW = 4
+KEYS = TOKENS // WINDOW
+SET = 128
+BLOCK = SET * WINDOW
+BLOCKS = BATCH * TOKENS // BLOCK
+BLOCKS_PER_BATCH = TOKENS // BLOCK
+PSUM_BANKS = 8
+PER_BANK = 2
+HALVES = 2
+SCORE_LAG = 2
+
+FLOPS = 2 * BATCH * TOKENS * D * D * 2 + 2 * BATCH * TOKENS * KEYS * D
+
+
+def tile_siglipsdpaattention_pa_t_kernel(tc, x, Wq, bq, Wk, bk, out):
+    nc = tc.nc
+    x_rows = x.flatten_outer_dims()
+    out_rows = out.flatten_outer_dims()
+
+    with ExitStack() as ctx:
+        ctx.enter_context(tc.manual_schedule())
+
+        const = ctx.enter_context(tc.tile_pool(name="const", bufs=1))
+        x_pool = ctx.enter_context(tc.tile_pool(name="x_pool", bufs=BLOCKS))
+        grouped_pool = ctx.enter_context(tc.tile_pool(name="grouped_pool", bufs=3))
+        x_mx_pool = ctx.enter_context(tc.tile_pool(name="x_mx_pool", bufs=3))
+        k_mx_pool = ctx.enter_context(tc.tile_pool(name="k_mx_pool", bufs=3))
+        q_mx_pool = ctx.enter_context(tc.tile_pool(name="q_mx_pool", bufs=SCORE_LAG + 2))
+        out_pool = ctx.enter_context(tc.tile_pool(name="out_pool", bufs=4))
+        psum = ctx.enter_context(tc.psum_pool(name="psum", bufs=PSUM_BANKS))
+
+        def mx_operand(pool, columns, label):
+            codes = pool.tile([P, columns], U32, name="%s_codes" % label, align_bytes=64)
+            scales = pool.tile([P, columns], U8, name="%s_scales" % label, align_bytes=64)
+            return codes, scales
+
+        def quantise(grouped, operand, columns):
+            codes, scales = operand
+            nc.vector.quantize_mx(
+                out=codes[:, columns].bitcast(FP8X4), scales=scales[:, columns], in_=grouped
+            )
+
+        def mx_pass(acc, stationary, stationary_columns, moving, moving_columns, start=True, stop=True):
+            nc.tensor.matmul_mx(
+                out=acc,
+                lhsT=stationary[0][:, stationary_columns].bitcast(FP8X4),
+                lhsT_scale=stationary[1][:, stationary_columns],
+                rhs=moving[0][:, moving_columns].bitcast(FP8X4),
+                rhs_scale=moving[1][:, moving_columns],
+                start=start,
+                stop=stop,
+            )
+
+        def sets(first, count=1):
+            return slice(first * SET, (first + count) * SET)
+
+        def load_four_rows_a_partition(rows, rows_sb):
+            nc.sync.dma_start(out=rows_sb[:], in_=rows.rearrange("(p s) d -> p (s d)", s=PACK))
+
+        wq_sb = const.tile([P, PACK * D], BF16)
+        wk_sb = const.tile([P, PACK * D], BF16)
+        load_four_rows_a_partition(Wq, wq_sb)
+        load_four_rows_a_partition(Wk, wk_sb)
+        x_sb = []
+        for n in range(BLOCKS):
+            x_block = x_pool.tile([P, PACK * D], BF16, name="x_block")
+            load_four_rows_a_partition(x_rows[n * BLOCK : (n + 1) * BLOCK, :], x_block)
+            x_sb.append(x_block)
+
+        bq_bf = const.tile([P, PACK], BF16)
+        bk_bf = const.tile([P, PACK], BF16)
+        nc.scalar.dma_start(out=bq_bf[:], in_=bq.rearrange("(p j) -> p j", j=PACK))
+        nc.scalar.dma_start(out=bk_bf[:], in_=bk.rearrange("(p j) -> p j", j=PACK))
+
+        ident = const.tile([P, P], F32)
+        make_identity(nc, ident[:])
+
+        def features_to_partitions(rows_sb, grouped, copy_out):
+            pairs = rows_sb[:].bitcast(F32)
+            grouped_pairs = grouped[:].bitcast(F32).rearrange("p (c u) -> p c u", u=HALVES)
+            for bank in range(PACK // PER_BANK):
+                flipped = psum.tile([P, HALVES, PER_BANK * SET], F32, name="flipped", tag="bank")
+                for i in range(PER_BANK):
+                    s = PER_BANK * bank + i
+                    for u in range(HALVES):
+                        every_second = slice(s * HALVES * P + u, (s + 1) * HALVES * P, HALVES)
+                        nc.tensor.transpose(flipped[:, u, sets(i)], pairs[:, every_second], ident[:])
+                copy_out(
+                    out=grouped_pairs[:, sets(PER_BANK * bank, PER_BANK), :],
+                    in_=flipped[:].rearrange("p u c -> p c u"),
+                )
+
+        wq_grouped = const.tile([P, PACK * D], BF16, align_bytes=64)
+        wk_grouped = const.tile([P, PACK * D], BF16, align_bytes=64)
+        features_to_partitions(wq_sb, wq_grouped, nc.vector.tensor_copy)
+        features_to_partitions(wk_sb, wk_grouped, nc.vector.tensor_copy)
+        wq_mx = mx_operand(const, D, "wq")
+        wk_mx = mx_operand(const, D, "wk")
+        quantise(wq_grouped[:], wq_mx, sets(0, PACK))
+        quantise(wk_grouped[:], wk_mx, sets(0, PACK))
+
+        bq_f32 = const.tile([P, PACK], F32)
+        bk_f32 = const.tile([P, PACK], F32)
+        nc.vector.tensor_copy(out=bq_f32[:], in_=bq_bf[:])
+        nc.vector.tensor_copy(out=bk_f32[:], in_=bk_bf[:])
+        bq_every_column = bq_f32[:].unsqueeze(1).to_broadcast([P, SET, PACK])
+        bk_every_column = bk_f32[:].unsqueeze(1).to_broadcast([P, SET, PACK])
+
+        x_mx = {}
+        q_grouped = {}
+        q_mx = {}
+        k_grouped = {}
+        k_mx = {}
+
+        def prepare_x(n):
+            x_grouped = grouped_pool.tile([P, PACK * BLOCK], BF16, name="x_grouped", align_bytes=64)
+            features_to_partitions(x_sb[n], x_grouped, nc.scalar.copy)
+            x_mx[n] = mx_operand(x_mx_pool, BLOCK, "x")
+            quantise(x_grouped[:], x_mx[n], sets(0, WINDOW))
+
+        def q_of_sets_2_and_3(n):
+            q_grouped[n] = grouped_pool.tile([P, BLOCK, PACK], BF16, name="q_grouped", align_bytes=64)
+            q_planes = grouped_pool.tile([P, PACK, 2 * SET], BF16, name="q_planes")
+            for bank in range(PACK // PER_BANK):
+                q_acc = psum.tile([P, PER_BANK, 2 * SET], F32, name="q_acc_planes", tag="bank")
+                for i in range(PER_BANK):
+                    mx_pass(q_acc[:, i, :], wq_mx, sets(PER_BANK * bank + i), x_mx[n], sets(2, 2))
+                for i in range(PER_BANK):
+                    j = PER_BANK * bank + i
+                    nc.scalar.activation(
+                        out=q_planes[:, j, :], in_=q_acc[:, i, :], func=IDENTITY,
+                        bias=bq_f32[:, j : j + 1], scale=1.0,
+                    )
+            nc.gpsimd.tensor_scalar(
+                out=q_grouped[n][:, sets(2, 2), :], in0=q_planes[:].rearrange("p j c -> p c j"),
+                scalar1=1.0, scalar2=0.0, op0=MULT, op1=ADD,
+            )
+
+        def q_of_sets_0_and_1(n):
+            for r in range(2):
+                q_acc = psum.tile([P, PACK, SET], F32, name="q_acc", tag="bank")
+                for j in range(PACK):
+                    mx_pass(q_acc[:, j, :], wq_mx, sets(j), x_mx[n], sets(r))
+                nc.vector.tensor_tensor(
+                    out=q_grouped[n][:, sets(r), :], in0=q_acc[:].rearrange("p j c -> p c j"),
+                    in1=bq_every_column, op=ADD,
+                )
+
+        def quantise_q(n):
+            q_mx[n] = mx_operand(q_mx_pool, BLOCK, "q")
+            quantise(q_grouped[n][:].rearrange("p c j -> p (c j)"), q_mx[n], sets(0, WINDOW))
+
+        def merged_k(n):
+            k_acc = psum.tile([P, PACK, SET], F32, name="k_acc", tag="bank")
+            for j in range(PACK):
+                for r in range(WINDOW):
+                    mx_pass(
+                        k_acc[:, j, :], wk_mx, sets(j), x_mx[n], sets(r),
+                        start=(r == 0), stop=(r == WINDOW - 1),
+                    )
+            k_grouped[n] = grouped_pool.tile([P, SET, PACK], BF16, name="k_grouped", align_bytes=64)
+            nc.vector.scalar_tensor_tensor(
+                out=k_grouped[n][:], in0=k_acc[:].rearrange("p j m -> p m j"), scalar=1.0 / WINDOW,
+                in1=bk_every_column, op0=MULT, op1=ADD,
+            )
+
+        def quantise_k(n):
+            b, part = divmod(n, BLOCKS_PER_BATCH)
+            if part == 0:
+                k_mx[b] = mx_operand(k_mx_pool, KEYS, "k")
+            quantise(k_grouped[n][:].rearrange("p m j -> p (m j)"), k_mx[b], sets(part))
+
+        def scores(n):
+            block_rows = out_rows[n * BLOCK : (n + 1) * BLOCK, :].rearrange("(m r) k -> m r k", r=WINDOW)
+            keys_mx = k_mx[n // BLOCKS_PER_BATCH]
+            for bank in range(WINDOW // PER_BANK):
+                score_acc = psum.tile([P, PER_BANK, KEYS], F32, name="score_acc", tag="bank")
+                for i in range(PER_BANK):
+                    mx_pass(score_acc[:, i, :], q_mx[n], sets(PER_BANK * bank + i), keys_mx, sets(0, 2))
+                logits = out_pool.tile([P, PER_BANK, KEYS], F32, name="logits")
+                nc.scalar.activation(
+                    out=logits[:], in_=score_acc[:], func=COPY,
+                    bias=math.log(WINDOW), scale=1.0 / math.sqrt(D),
+                )
+                nc.sync.dma_start(
+                    out=block_rows[:, PER_BANK * bank : PER_BANK * (bank + 1), :], in_=logits[:]
+                )
+
+        prepare_x(0)
+        for n in range(BLOCKS + SCORE_LAG):
+            if n + 1 < BLOCKS:
+                prepare_x(n + 1)
+            if 1 <= n <= BLOCKS:
+                quantise_q(n - 1)
+            if n < BLOCKS:
+                q_of_sets_2_and_3(n)
+                merged_k(n)
+            if n >= SCORE_LAG:
+                scores(n - SCORE_LAG)
+            if n < BLOCKS:
+                q_of_sets_0_and_1(n)
+                quantise_k(n)

@@ -27,6 +27,7 @@ BLOCKS = BATCH * TOKENS // BLOCK
 BLOCKS_PER_BATCH = TOKENS // BLOCK
 PSUM_BANKS = 8
 PER_BANK = 2
+RUN = 16
 HALVES = 2
 SCORE_LAG = 2
 
@@ -44,6 +45,7 @@ def tile_siglipsdpaattention_pa_t_kernel(tc, x, Wq, bq, Wk, bk, out):
         const = ctx.enter_context(tc.tile_pool(name="const", bufs=1))
         x_pool = ctx.enter_context(tc.tile_pool(name="x_pool", bufs=BLOCKS))
         grouped_pool = ctx.enter_context(tc.tile_pool(name="grouped_pool", bufs=3))
+        ordered_pool = ctx.enter_context(tc.tile_pool(name="ordered_pool", bufs=3))
         x_mx_pool = ctx.enter_context(tc.tile_pool(name="x_mx_pool", bufs=3))
         k_mx_pool = ctx.enter_context(tc.tile_pool(name="k_mx_pool", bufs=3))
         q_mx_pool = ctx.enter_context(tc.tile_pool(name="q_mx_pool", bufs=SCORE_LAG + 2))
@@ -96,16 +98,24 @@ def tile_siglipsdpaattention_pa_t_kernel(tc, x, Wq, bq, Wk, bk, out):
         ident = const.tile([P, P], F32)
         make_identity(nc, ident[:])
 
-        def features_to_partitions(rows_sb, grouped, copy_out):
-            pairs = rows_sb[:].bitcast(F32)
+        def order_runs(rows_sb):
+            ordered = ordered_pool.tile([P, HALVES, PACK, D // HALVES], BF16, name="ordered")
+            nc.vector.tensor_copy(
+                out=ordered[:].rearrange("p u s (g i) -> p u (s g) i", i=RUN),
+                in_=rows_sb[:].rearrange("p (sg u i) -> p u sg i", u=HALVES, i=RUN),
+            )
+            return ordered
+
+        def features_to_partitions(ordered, grouped, copy_out):
+            pairs = ordered[:].rearrange("p u s k -> p (u s k)").bitcast(F32)
             grouped_pairs = grouped[:].bitcast(F32).rearrange("p (c u) -> p c u", u=HALVES)
             for bank in range(PACK // PER_BANK):
                 flipped = psum.tile([P, HALVES, PER_BANK * SET], F32, name="flipped", tag="bank")
                 for i in range(PER_BANK):
                     s = PER_BANK * bank + i
                     for u in range(HALVES):
-                        every_second = slice(s * HALVES * P + u, (s + 1) * HALVES * P, HALVES)
-                        nc.tensor.transpose(flipped[:, u, sets(i)], pairs[:, every_second], ident[:])
+                        first = (u * PACK + s) * P
+                        nc.tensor.transpose(flipped[:, u, sets(i)], pairs[:, first : first + P], ident[:])
                 copy_out(
                     out=grouped_pairs[:, sets(PER_BANK * bank, PER_BANK), :],
                     in_=flipped[:].rearrange("p u c -> p c u"),
@@ -113,8 +123,10 @@ def tile_siglipsdpaattention_pa_t_kernel(tc, x, Wq, bq, Wk, bk, out):
 
         wq_grouped = const.tile([P, PACK * D], BF16, align_bytes=64)
         wk_grouped = const.tile([P, PACK * D], BF16, align_bytes=64)
-        features_to_partitions(wq_sb, wq_grouped, nc.vector.tensor_copy)
-        features_to_partitions(wk_sb, wk_grouped, nc.vector.tensor_copy)
+        wq_ordered = order_runs(wq_sb)
+        wk_ordered = order_runs(wk_sb)
+        features_to_partitions(wq_ordered, wq_grouped, nc.vector.tensor_copy)
+        features_to_partitions(wk_ordered, wk_grouped, nc.vector.tensor_copy)
         wq_mx = mx_operand(const, D, "wq")
         wk_mx = mx_operand(const, D, "wk")
         quantise(wq_grouped[:], wq_mx, sets(0, PACK))
@@ -127,6 +139,7 @@ def tile_siglipsdpaattention_pa_t_kernel(tc, x, Wq, bq, Wk, bk, out):
         bq_every_column = bq_f32[:].unsqueeze(1).to_broadcast([P, SET, PACK])
         bk_every_column = bk_f32[:].unsqueeze(1).to_broadcast([P, SET, PACK])
 
+        x_ordered = {}
         x_mx = {}
         q_grouped = {}
         q_mx = {}
@@ -135,7 +148,7 @@ def tile_siglipsdpaattention_pa_t_kernel(tc, x, Wq, bq, Wk, bk, out):
 
         def prepare_x(n):
             x_grouped = grouped_pool.tile([P, PACK * BLOCK], BF16, name="x_grouped", align_bytes=64)
-            features_to_partitions(x_sb[n], x_grouped, nc.scalar.copy)
+            features_to_partitions(x_ordered[n], x_grouped, nc.scalar.copy)
             x_mx[n] = mx_operand(x_mx_pool, BLOCK, "x")
             quantise(x_grouped[:], x_mx[n], sets(0, WINDOW))
 
@@ -207,12 +220,16 @@ def tile_siglipsdpaattention_pa_t_kernel(tc, x, Wq, bq, Wk, bk, out):
                     out=block_rows[:, PER_BANK * bank : PER_BANK * (bank + 1), :], in_=logits[:]
                 )
 
+        x_ordered[0] = order_runs(x_sb[0])
+        x_ordered[1] = order_runs(x_sb[1])
         prepare_x(0)
         for n in range(BLOCKS + SCORE_LAG):
             if n + 1 < BLOCKS:
                 prepare_x(n + 1)
             if 1 <= n <= BLOCKS:
                 quantise_q(n - 1)
+            if n + 2 < BLOCKS:
+                x_ordered[n + 2] = order_runs(x_sb[n + 2])
             if n < BLOCKS:
                 q_of_sets_2_and_3(n)
                 merged_k(n)

@@ -24,9 +24,11 @@ KEYS = TOKENS // WINDOW
 SET = 128
 BLOCK = SET * WINDOW
 BLOCKS = BATCH * TOKENS // BLOCK
+LAST = BLOCKS - 1
 BLOCKS_PER_BATCH = TOKENS // BLOCK
 PSUM_BANKS = 8
 PER_BANK = 2
+BANKS = PACK // PER_BANK
 RUN = 16
 HALVES = 2
 SCORE_LAG = 2
@@ -44,8 +46,8 @@ def tile_siglipsdpaattention_pa_t_kernel(tc, x, Wq, bq, Wk, bk, out):
 
         const = ctx.enter_context(tc.tile_pool(name="const", bufs=1))
         x_pool = ctx.enter_context(tc.tile_pool(name="x_pool", bufs=BLOCKS))
-        grouped_pool = ctx.enter_context(tc.tile_pool(name="grouped_pool", bufs=3))
         ordered_pool = ctx.enter_context(tc.tile_pool(name="ordered_pool", bufs=3))
+        grouped_pool = ctx.enter_context(tc.tile_pool(name="grouped_pool", bufs=3))
         x_mx_pool = ctx.enter_context(tc.tile_pool(name="x_mx_pool", bufs=3))
         k_mx_pool = ctx.enter_context(tc.tile_pool(name="k_mx_pool", bufs=3))
         q_mx_pool = ctx.enter_context(tc.tile_pool(name="q_mx_pool", bufs=SCORE_LAG + 2))
@@ -77,18 +79,23 @@ def tile_siglipsdpaattention_pa_t_kernel(tc, x, Wq, bq, Wk, bk, out):
         def sets(first, count=1):
             return slice(first * SET, (first + count) * SET)
 
-        def load_four_rows_a_partition(rows, rows_sb):
-            nc.sync.dma_start(out=rows_sb[:], in_=rows.rearrange("(p s) d -> p (s d)", s=PACK))
+        def load_rows(rows, rows_sb, pieces=1):
+            rows = rows.rearrange("(p s) d -> p s d", s=PACK)
+            for piece in range(pieces):
+                slots = slice(piece * PACK // pieces, (piece + 1) * PACK // pieces)
+                nc.sync.dma_start(out=rows_sb[:, slots, :], in_=rows[:, slots, :])
 
-        wq_sb = const.tile([P, PACK * D], BF16)
-        wk_sb = const.tile([P, PACK * D], BF16)
-        load_four_rows_a_partition(Wq, wq_sb)
-        load_four_rows_a_partition(Wk, wk_sb)
-        x_sb = []
-        for n in range(BLOCKS):
-            x_block = x_pool.tile([P, PACK * D], BF16, name="x_block")
-            load_four_rows_a_partition(x_rows[n * BLOCK : (n + 1) * BLOCK, :], x_block)
-            x_sb.append(x_block)
+        def x_block(n):
+            return x_rows[n * BLOCK : (n + 1) * BLOCK, :]
+
+        wq_sb = const.tile([P, PACK, D], BF16)
+        wk_sb = const.tile([P, PACK, D], BF16)
+        x_sb = [x_pool.tile([P, PACK, D], BF16, name="x_sb") for n in range(BLOCKS)]
+        load_rows(Wq, wq_sb, pieces=2)
+        load_rows(x_block(0), x_sb[0], pieces=2)
+        load_rows(Wk, wk_sb)
+        for n in range(1, BLOCKS):
+            load_rows(x_block(n), x_sb[n])
 
         bq_bf = const.tile([P, PACK], BF16)
         bk_bf = const.tile([P, PACK], BF16)
@@ -98,64 +105,97 @@ def tile_siglipsdpaattention_pa_t_kernel(tc, x, Wq, bq, Wk, bk, out):
         ident = const.tile([P, P], F32)
         make_identity(nc, ident[:])
 
-        def order_runs(rows_sb):
-            ordered = ordered_pool.tile([P, HALVES, PACK, D // HALVES], BF16, name="ordered")
-            nc.vector.tensor_copy(
-                out=ordered[:].rearrange("p u s (g i) -> p u (s g) i", i=RUN),
-                in_=rows_sb[:].rearrange("p (sg u i) -> p u sg i", u=HALVES, i=RUN),
-            )
-            return ordered
+        def new_ordered():
+            return ordered_pool.tile([P, HALVES, PACK, D // HALVES], BF16, name="ordered")
 
-        def features_to_partitions(ordered, grouped, copy_out):
+        def order_runs(rows_sb, ordered, first=0, count=PACK):
+            slots = slice(first, first + count)
+            nc.vector.tensor_copy(
+                out=ordered[:, :, slots, :].rearrange("p u s (g i) -> p u (s g) i", i=RUN),
+                in_=rows_sb[:, slots, :].rearrange("p s (g u i) -> p u (s g) i", u=HALVES, i=RUN),
+            )
+
+        def bank_to_partitions(ordered, grouped, bank, copy_out):
             pairs = ordered[:].rearrange("p u s k -> p (u s k)").bitcast(F32)
             grouped_pairs = grouped[:].bitcast(F32).rearrange("p (c u) -> p c u", u=HALVES)
-            for bank in range(PACK // PER_BANK):
-                flipped = psum.tile([P, HALVES, PER_BANK * SET], F32, name="flipped", tag="bank")
-                for i in range(PER_BANK):
-                    s = PER_BANK * bank + i
-                    for u in range(HALVES):
-                        first = (u * PACK + s) * P
-                        nc.tensor.transpose(flipped[:, u, sets(i)], pairs[:, first : first + P], ident[:])
-                copy_out(
-                    out=grouped_pairs[:, sets(PER_BANK * bank, PER_BANK), :],
-                    in_=flipped[:].rearrange("p u c -> p c u"),
-                )
-
-        wq_grouped = const.tile([P, PACK * D], BF16, align_bytes=64)
-        wk_grouped = const.tile([P, PACK * D], BF16, align_bytes=64)
-        wq_ordered = order_runs(wq_sb)
-        wk_ordered = order_runs(wk_sb)
-        features_to_partitions(wq_ordered, wq_grouped, nc.vector.tensor_copy)
-        features_to_partitions(wk_ordered, wk_grouped, nc.vector.tensor_copy)
-        wq_mx = mx_operand(const, D, "wq")
-        wk_mx = mx_operand(const, D, "wk")
-        quantise(wq_grouped[:], wq_mx, sets(0, PACK))
-        quantise(wk_grouped[:], wk_mx, sets(0, PACK))
+            flipped = psum.tile([P, HALVES, PER_BANK * SET], F32, name="flipped", tag="bank")
+            for i in range(PER_BANK):
+                for u in range(HALVES):
+                    first = (u * PACK + PER_BANK * bank + i) * P
+                    nc.tensor.transpose(flipped[:, u, sets(i)], pairs[:, first : first + P], ident[:])
+            copy_out(
+                out=grouped_pairs[:, sets(PER_BANK * bank, PER_BANK), :],
+                in_=flipped[:].rearrange("p u c -> p c u"),
+            )
 
         bq_f32 = const.tile([P, PACK], F32)
         bk_f32 = const.tile([P, PACK], F32)
+
+        wq_grouped = const.tile([P, PACK * D], BF16, align_bytes=64)
+        wk_grouped = const.tile([P, PACK * D], BF16, align_bytes=64)
+        wq_mx = mx_operand(const, D, "wq")
+        wk_mx = mx_operand(const, D, "wk")
+        wq_ordered = const.tile([P, HALVES, PACK, D // HALVES], BF16)
+        wk_ordered = const.tile([P, HALVES, PACK, D // HALVES], BF16)
+        x_ordered = {}
+        x_mx = {}
+
+        def new_x_grouped():
+            return grouped_pool.tile([P, PACK * BLOCK], BF16, name="x_grouped", align_bytes=64)
+
+        def quantise_x(n, x_grouped):
+            x_mx[n] = mx_operand(x_mx_pool, BLOCK, "x")
+            quantise(x_grouped[:], x_mx[n], sets(0, WINDOW))
+
+        def order_x(n):
+            x_ordered[n] = new_ordered()
+            order_runs(x_sb[n], x_ordered[n])
+
+        x_ordered[0] = new_ordered()
+        for bank in range(BANKS):
+            order_runs(wq_sb, wq_ordered, PER_BANK * bank, PER_BANK)
+        for bank in range(BANKS):
+            order_runs(x_sb[0], x_ordered[0], PER_BANK * bank, PER_BANK)
+        first_x_grouped = new_x_grouped()
+        for bank in range(BANKS):
+            bank_to_partitions(wq_ordered, wq_grouped, bank, nc.vector.tensor_copy)
+        for bank in range(BANKS):
+            bank_to_partitions(x_ordered[0], first_x_grouped, bank, nc.scalar.copy)
+        quantise(wq_grouped[:], wq_mx, sets(0, PACK))
+        order_runs(wk_sb, wk_ordered)
+        quantise_x(0, first_x_grouped)
+        order_x(1)
+        for bank in range(BANKS):
+            bank_to_partitions(wk_ordered, wk_grouped, bank, nc.scalar.copy)
+        quantise(wk_grouped[:], wk_mx, sets(0, PACK))
         nc.vector.tensor_copy(out=bq_f32[:], in_=bq_bf[:])
         nc.vector.tensor_copy(out=bk_f32[:], in_=bk_bf[:])
+        order_x(2)
+
         bq_every_column = bq_f32[:].unsqueeze(1).to_broadcast([P, SET, PACK])
         bk_every_column = bk_f32[:].unsqueeze(1).to_broadcast([P, SET, PACK])
 
-        x_ordered = {}
-        x_mx = {}
         q_grouped = {}
         q_mx = {}
         k_grouped = {}
         k_mx = {}
 
         def prepare_x(n):
-            x_grouped = grouped_pool.tile([P, PACK * BLOCK], BF16, name="x_grouped", align_bytes=64)
-            features_to_partitions(x_ordered[n], x_grouped, nc.scalar.copy)
-            x_mx[n] = mx_operand(x_mx_pool, BLOCK, "x")
-            quantise(x_grouped[:], x_mx[n], sets(0, WINDOW))
+            x_grouped = new_x_grouped()
+            for bank in range(BANKS):
+                bank_to_partitions(x_ordered[n], x_grouped, bank, nc.scalar.copy)
+            quantise_x(n, x_grouped)
 
-        def q_of_sets_2_and_3(n):
+        def new_q(n):
             q_grouped[n] = grouped_pool.tile([P, BLOCK, PACK], BF16, name="q_grouped", align_bytes=64)
+            q_mx[n] = mx_operand(q_mx_pool, BLOCK, "q")
+
+        def copy_on_gpsimd(out, in_):
+            nc.gpsimd.tensor_scalar(out=out, in0=in_, scalar1=1.0, scalar2=0.0, op0=MULT, op1=ADD)
+
+        def q_of_sets_2_and_3(n, interleave):
             q_planes = grouped_pool.tile([P, PACK, 2 * SET], BF16, name="q_planes")
-            for bank in range(PACK // PER_BANK):
+            for bank in range(BANKS):
                 q_acc = psum.tile([P, PER_BANK, 2 * SET], F32, name="q_acc_planes", tag="bank")
                 for i in range(PER_BANK):
                     mx_pass(q_acc[:, i, :], wq_mx, sets(PER_BANK * bank + i), x_mx[n], sets(2, 2))
@@ -165,10 +205,7 @@ def tile_siglipsdpaattention_pa_t_kernel(tc, x, Wq, bq, Wk, bk, out):
                         out=q_planes[:, j, :], in_=q_acc[:, i, :], func=IDENTITY,
                         bias=bq_f32[:, j : j + 1], scale=1.0,
                     )
-            nc.gpsimd.tensor_scalar(
-                out=q_grouped[n][:, sets(2, 2), :], in0=q_planes[:].rearrange("p j c -> p c j"),
-                scalar1=1.0, scalar2=0.0, op0=MULT, op1=ADD,
-            )
+            interleave(out=q_grouped[n][:, sets(2, 2), :], in_=q_planes[:].rearrange("p j c -> p c j"))
 
         def q_of_sets_0_and_1(n):
             for r in range(2):
@@ -180,9 +217,9 @@ def tile_siglipsdpaattention_pa_t_kernel(tc, x, Wq, bq, Wk, bk, out):
                     in1=bq_every_column, op=ADD,
                 )
 
-        def quantise_q(n):
-            q_mx[n] = mx_operand(q_mx_pool, BLOCK, "q")
-            quantise(q_grouped[n][:].rearrange("p c j -> p (c j)"), q_mx[n], sets(0, WINDOW))
+        def quantise_q(n, first=0, count=WINDOW):
+            columns = sets(first, count)
+            quantise(q_grouped[n][:, columns, :].rearrange("p c j -> p (c j)"), q_mx[n], columns)
 
         def merged_k(n):
             k_acc = psum.tile([P, PACK, SET], F32, name="k_acc", tag="bank")
@@ -204,37 +241,53 @@ def tile_siglipsdpaattention_pa_t_kernel(tc, x, Wq, bq, Wk, bk, out):
                 k_mx[b] = mx_operand(k_mx_pool, KEYS, "k")
             quantise(k_grouped[n][:].rearrange("p m j -> p (m j)"), k_mx[b], sets(part))
 
-        def scores(n):
-            block_rows = out_rows[n * BLOCK : (n + 1) * BLOCK, :].rearrange("(m r) k -> m r k", r=WINDOW)
-            keys_mx = k_mx[n // BLOCKS_PER_BATCH]
-            for bank in range(WINDOW // PER_BANK):
-                score_acc = psum.tile([P, PER_BANK, KEYS], F32, name="score_acc", tag="bank")
-                for i in range(PER_BANK):
-                    mx_pass(score_acc[:, i, :], q_mx[n], sets(PER_BANK * bank + i), keys_mx, sets(0, 2))
-                logits = out_pool.tile([P, PER_BANK, KEYS], F32, name="logits")
-                nc.scalar.activation(
-                    out=logits[:], in_=score_acc[:], func=COPY,
-                    bias=math.log(WINDOW), scale=1.0 / math.sqrt(D),
-                )
-                nc.sync.dma_start(
-                    out=block_rows[:, PER_BANK * bank : PER_BANK * (bank + 1), :], in_=logits[:]
-                )
+        def scale_on_scalar(out, in_):
+            nc.scalar.activation(
+                out=out, in_=in_, func=COPY, bias=math.log(WINDOW), scale=1.0 / math.sqrt(D)
+            )
 
-        x_ordered[0] = order_runs(x_sb[0])
-        x_ordered[1] = order_runs(x_sb[1])
-        prepare_x(0)
-        for n in range(BLOCKS + SCORE_LAG):
-            if n + 1 < BLOCKS:
-                prepare_x(n + 1)
-            if 1 <= n <= BLOCKS:
+        def scale_on_vector(out, in_):
+            nc.vector.tensor_scalar(
+                out=out, in0=in_, scalar1=1.0 / math.sqrt(D), scalar2=math.log(WINDOW),
+                op0=MULT, op1=ADD,
+            )
+
+        def scores(n, bank, scale):
+            block_rows = out_rows[n * BLOCK : (n + 1) * BLOCK, :].rearrange("(m r) k -> m r k", r=WINDOW)
+            first = PER_BANK * bank
+            score_acc = psum.tile([P, PER_BANK, KEYS], F32, name="score_acc", tag="bank")
+            for i in range(PER_BANK):
+                mx_pass(score_acc[:, i, :], q_mx[n], sets(first + i), k_mx[n // BLOCKS_PER_BATCH], sets(0, 2))
+            logits = out_pool.tile([P, PER_BANK, KEYS], F32, name="logits")
+            scale(out=logits[:], in_=score_acc[:])
+            nc.sync.dma_start(out=block_rows[:, first : first + PER_BANK, :], in_=logits[:])
+
+        for n in range(LAST):
+            prepare_x(n + 1)
+            if n > 0:
                 quantise_q(n - 1)
-            if n + 2 < BLOCKS:
-                x_ordered[n + 2] = order_runs(x_sb[n + 2])
-            if n < BLOCKS:
-                q_of_sets_2_and_3(n)
-                merged_k(n)
+            new_q(n)
+            q_of_sets_2_and_3(n, copy_on_gpsimd)
+            merged_k(n)
             if n >= SCORE_LAG:
-                scores(n - SCORE_LAG)
-            if n < BLOCKS:
-                q_of_sets_0_and_1(n)
-                quantise_k(n)
+                for bank in range(BANKS):
+                    scores(n - SCORE_LAG, bank, scale_on_scalar)
+            q_of_sets_0_and_1(n)
+            quantise_k(n)
+            if n + 3 < BLOCKS:
+                order_x(n + 3)
+
+        for bank in range(BANKS):
+            scores(LAST - 2, bank, scale_on_scalar)
+        quantise_q(LAST - 1)
+        merged_k(LAST)
+        quantise_k(LAST)
+        new_q(LAST)
+        q_of_sets_0_and_1(LAST)
+        quantise_q(LAST, 0, 2)
+        q_of_sets_2_and_3(LAST, nc.vector.tensor_copy)
+        quantise_q(LAST, 2, 2)
+        for bank in range(BANKS):
+            scores(LAST - 1, bank, scale_on_scalar)
+        scores(LAST, 0, scale_on_scalar)
+        scores(LAST, 1, scale_on_vector)

@@ -128,6 +128,14 @@ def tile_siglipsdpaattention_pa_t_kernel(tc, x, Wq, bq, Wk, bk, out):
                 in_=flipped[:].rearrange("p u c -> p c u"),
             )
 
+        zeros = const.tile([P, BLOCK], BF16)
+        nc.vector.memset(zeros[:], 0.0)
+
+        def raise_clock(count):
+            scrap = psum.tile([P, BLOCK], F32, name="scrap", tag="bank")
+            for i in range(count):
+                nc.tensor.matmul(scrap[:], lhsT=zeros[:, sets(0)], rhs=zeros[:], start=True, stop=True)
+
         bq_f32 = const.tile([P, PACK], F32)
         bk_f32 = const.tile([P, PACK], F32)
 
@@ -152,6 +160,7 @@ def tile_siglipsdpaattention_pa_t_kernel(tc, x, Wq, bq, Wk, bk, out):
             order_runs(x_sb[n], x_ordered[n])
 
         x_ordered[0] = new_ordered()
+        raise_clock(5)
         for bank in range(BANKS):
             order_runs(wq_sb, wq_ordered, PER_BANK * bank, PER_BANK)
         for bank in range(BANKS):
@@ -159,14 +168,17 @@ def tile_siglipsdpaattention_pa_t_kernel(tc, x, Wq, bq, Wk, bk, out):
         first_x_grouped = new_x_grouped()
         for bank in range(BANKS):
             bank_to_partitions(wq_ordered, wq_grouped, bank, nc.vector.tensor_copy)
+        raise_clock(2)
         for bank in range(BANKS):
             bank_to_partitions(x_ordered[0], first_x_grouped, bank, nc.scalar.copy)
+        raise_clock(2)
         quantise(wq_grouped[:], wq_mx, sets(0, PACK))
         order_runs(wk_sb, wk_ordered)
         quantise_x(0, first_x_grouped)
         order_x(1)
         for bank in range(BANKS):
             bank_to_partitions(wk_ordered, wk_grouped, bank, nc.scalar.copy)
+        raise_clock(2)
         quantise(wk_grouped[:], wk_mx, sets(0, PACK))
         nc.vector.tensor_copy(out=bq_f32[:], in_=bq_bf[:])
         nc.vector.tensor_copy(out=bk_f32[:], in_=bk_bf[:])

@@ -165,9 +165,11 @@ def tile_siglipsdpaattention_pa_t_kernel(tc, x, Wq, bq, Wk, bk, out):
             order_runs(wq_sb, wq_ordered, PER_BANK * bank, PER_BANK)
         for bank in range(BANKS):
             order_runs(x_sb[0], x_ordered[0], PER_BANK * bank, PER_BANK)
+        nc.vector.tensor_copy(out=bq_f32[:], in_=bq_bf[:])
+        nc.vector.tensor_copy(out=bk_f32[:], in_=bk_bf[:])
         first_x_grouped = new_x_grouped()
         for bank in range(BANKS):
-            bank_to_partitions(wq_ordered, wq_grouped, bank, nc.vector.tensor_copy)
+            bank_to_partitions(wq_ordered, wq_grouped, bank, nc.scalar.copy)
         raise_clock(2)
         for bank in range(BANKS):
             bank_to_partitions(x_ordered[0], first_x_grouped, bank, nc.scalar.copy)
@@ -178,10 +180,7 @@ def tile_siglipsdpaattention_pa_t_kernel(tc, x, Wq, bq, Wk, bk, out):
         order_x(1)
         for bank in range(BANKS):
             bank_to_partitions(wk_ordered, wk_grouped, bank, nc.scalar.copy)
-        raise_clock(2)
         quantise(wk_grouped[:], wk_mx, sets(0, PACK))
-        nc.vector.tensor_copy(out=bq_f32[:], in_=bq_bf[:])
-        nc.vector.tensor_copy(out=bk_f32[:], in_=bk_bf[:])
         order_x(2)
 
         bq_every_column = bq_f32[:].unsqueeze(1).to_broadcast([P, SET, PACK])
@@ -274,10 +273,16 @@ def tile_siglipsdpaattention_pa_t_kernel(tc, x, Wq, bq, Wk, bk, out):
             scale(out=logits[:], in_=score_acc[:])
             nc.sync.dma_start(out=block_rows[:, first : first + PER_BANK, :], in_=logits[:])
 
-        for n in range(LAST):
+        new_q(0)
+        q_of_sets_2_and_3(0, copy_on_gpsimd)
+        q_of_sets_0_and_1(0)
+        prepare_x(1)
+        merged_k(0)
+        quantise_k(0)
+        order_x(3)
+        for n in range(1, LAST):
             prepare_x(n + 1)
-            if n > 0:
-                quantise_q(n - 1)
+            quantise_q(n - 1)
             new_q(n)
             q_of_sets_2_and_3(n, copy_on_gpsimd)
             merged_k(n)
@@ -289,15 +294,15 @@ def tile_siglipsdpaattention_pa_t_kernel(tc, x, Wq, bq, Wk, bk, out):
             if n + 3 < BLOCKS:
                 order_x(n + 3)
 
-        for bank in range(BANKS):
-            scores(LAST - 2, bank, scale_on_scalar)
         quantise_q(LAST - 1)
         merged_k(LAST)
-        quantise_k(LAST)
         new_q(LAST)
+        q_of_sets_2_and_3(LAST, copy_on_gpsimd)
+        for bank in range(BANKS):
+            scores(LAST - 2, bank, scale_on_scalar)
+        quantise_k(LAST)
         q_of_sets_0_and_1(LAST)
         quantise_q(LAST, 0, 2)
-        q_of_sets_2_and_3(LAST, nc.vector.tensor_copy)
         quantise_q(LAST, 2, 2)
         for bank in range(BANKS):
             scores(LAST - 1, bank, scale_on_scalar)

@@ -29,8 +29,8 @@ BLOCKS_PER_BATCH = TOKENS // BLOCK
 PSUM_BANKS = 8
 PER_BANK = 2
 BANKS = PACK // PER_BANK
-RUN = 16
 HALVES = 2
+DIRECT = 1
 SCORE_LAG = 2
 
 FLOPS = 2 * BATCH * TOKENS * D * D * 2 + 2 * BATCH * TOKENS * KEYS * D
@@ -105,24 +105,25 @@ def tile_siglipsdpaattention_pa_t_kernel(tc, x, Wq, bq, Wk, bk, out):
         ident = const.tile([P, P], F32)
         make_identity(nc, ident[:])
 
-        def new_ordered():
-            return ordered_pool.tile([P, HALVES, PACK, D // HALVES], BF16, name="ordered")
-
-        def order_runs(rows_sb, ordered, first=0, count=PACK):
-            slots = slice(first, first + count)
+        def order_pairs(rows_sb):
+            ordered = ordered_pool.tile([P, HALVES, PACK, P], F32, name="ordered")
             nc.vector.tensor_copy(
-                out=ordered[:, :, slots, :].rearrange("p u s (g i) -> p u (s g) i", i=RUN),
-                in_=rows_sb[:, slots, :].rearrange("p s (g u i) -> p u (s g) i", u=HALVES, i=RUN),
+                out=ordered[:], in_=rows_sb[:].bitcast(F32).rearrange("p s (q u) -> p u s q", u=HALVES)
             )
+            return ordered
 
-        def bank_to_partitions(ordered, grouped, bank, copy_out):
-            pairs = ordered[:].rearrange("p u s k -> p (u s k)").bitcast(F32)
+        def in_order(ordered):
+            return lambda s, u: ordered[:, u, s, :]
+
+        def every_second(rows_sb):
+            return lambda s, u: rows_sb[:, s, :].bitcast(F32)[:, u::HALVES]
+
+        def bank_to_partitions(pairs, grouped, bank, copy_out):
             grouped_pairs = grouped[:].bitcast(F32).rearrange("p (c u) -> p c u", u=HALVES)
             flipped = psum.tile([P, HALVES, PER_BANK * SET], F32, name="flipped", tag="bank")
             for i in range(PER_BANK):
                 for u in range(HALVES):
-                    first = (u * PACK + PER_BANK * bank + i) * P
-                    nc.tensor.transpose(flipped[:, u, sets(i)], pairs[:, first : first + P], ident[:])
+                    nc.tensor.transpose(flipped[:, u, sets(i)], pairs(PER_BANK * bank + i, u), ident[:])
             copy_out(
                 out=grouped_pairs[:, sets(PER_BANK * bank, PER_BANK), :],
                 in_=flipped[:].rearrange("p u c -> p c u"),
@@ -143,9 +144,7 @@ def tile_siglipsdpaattention_pa_t_kernel(tc, x, Wq, bq, Wk, bk, out):
         wk_grouped = const.tile([P, PACK * D], BF16, align_bytes=64)
         wq_mx = mx_operand(const, D, "wq")
         wk_mx = mx_operand(const, D, "wk")
-        wq_ordered = const.tile([P, HALVES, PACK, D // HALVES], BF16)
-        wk_ordered = const.tile([P, HALVES, PACK, D // HALVES], BF16)
-        x_ordered = {}
+        x_pairs = {}
         x_mx = {}
 
         def new_x_grouped():
@@ -156,30 +155,25 @@ def tile_siglipsdpaattention_pa_t_kernel(tc, x, Wq, bq, Wk, bk, out):
             quantise(x_grouped[:], x_mx[n], sets(0, WINDOW))
 
         def order_x(n):
-            x_ordered[n] = new_ordered()
-            order_runs(x_sb[n], x_ordered[n])
+            x_pairs[n] = in_order(order_pairs(x_sb[n]))
 
-        x_ordered[0] = new_ordered()
-        raise_clock(5)
-        for bank in range(BANKS):
-            order_runs(wq_sb, wq_ordered, PER_BANK * bank, PER_BANK)
-        for bank in range(BANKS):
-            order_runs(x_sb[0], x_ordered[0], PER_BANK * bank, PER_BANK)
+        for n in range(DIRECT):
+            x_pairs[n] = every_second(x_sb[n])
+        raise_clock(3)
         nc.vector.tensor_copy(out=bq_f32[:], in_=bq_bf[:])
         nc.vector.tensor_copy(out=bk_f32[:], in_=bk_bf[:])
         first_x_grouped = new_x_grouped()
+        copies = (nc.scalar.copy, nc.vector.tensor_copy)
         for bank in range(BANKS):
-            bank_to_partitions(wq_ordered, wq_grouped, bank, nc.scalar.copy)
-        raise_clock(2)
-        for bank in range(BANKS):
-            bank_to_partitions(x_ordered[0], first_x_grouped, bank, nc.scalar.copy)
-        raise_clock(2)
+            bank_to_partitions(every_second(wq_sb), wq_grouped, bank, copies[bank])
         quantise(wq_grouped[:], wq_mx, sets(0, PACK))
-        order_runs(wk_sb, wk_ordered)
-        quantise_x(0, first_x_grouped)
-        order_x(1)
         for bank in range(BANKS):
-            bank_to_partitions(wk_ordered, wk_grouped, bank, nc.scalar.copy)
+            bank_to_partitions(x_pairs[0], first_x_grouped, bank, nc.scalar.copy)
+        raise_clock(2)
+        quantise_x(0, first_x_grouped)
+        for bank in range(BANKS):
+            bank_to_partitions(every_second(wk_sb), wk_grouped, bank, nc.scalar.copy)
+        order_x(1)
         quantise(wk_grouped[:], wk_mx, sets(0, PACK))
         order_x(2)
 
@@ -194,7 +188,7 @@ def tile_siglipsdpaattention_pa_t_kernel(tc, x, Wq, bq, Wk, bk, out):
         def prepare_x(n):
             x_grouped = new_x_grouped()
             for bank in range(BANKS):
-                bank_to_partitions(x_ordered[n], x_grouped, bank, nc.scalar.copy)
+                bank_to_partitions(x_pairs[n], x_grouped, bank, nc.scalar.copy)
             quantise_x(n, x_grouped)
 
         def new_q(n):
@@ -295,16 +289,16 @@ def tile_siglipsdpaattention_pa_t_kernel(tc, x, Wq, bq, Wk, bk, out):
                 order_x(n + 3)
 
         quantise_q(LAST - 1)
-        merged_k(LAST)
         new_q(LAST)
         q_of_sets_2_and_3(LAST, copy_on_gpsimd)
+        merged_k(LAST)
         for bank in range(BANKS):
             scores(LAST - 2, bank, scale_on_scalar)
         quantise_k(LAST)
         q_of_sets_0_and_1(LAST)
-        quantise_q(LAST, 0, 2)
-        quantise_q(LAST, 2, 2)
         for bank in range(BANKS):
             scores(LAST - 1, bank, scale_on_scalar)
-        scores(LAST, 0, scale_on_scalar)
+        quantise_q(LAST, 2, 2)
+        quantise_q(LAST, 0, 2)
         scores(LAST, 1, scale_on_vector)
+        scores(LAST, 0, scale_on_scalar)

import math
from contextlib import ExitStack

import concourse.mybir as mybir
from concourse.masks import make_identity

F32 = mybir.dt.float32
BF16 = mybir.dt.bfloat16
U32 = mybir.dt.uint32
U8 = mybir.dt.uint8
FP8X4 = mybir.dt.float8_e4m3fn_x4
ADD = mybir.AluOpType.add
MULT = mybir.AluOpType.mult
IDENTITY = mybir.ActivationFunctionType.Identity
COPY = mybir.ActivationFunctionType.Copy

P = 128
PACK = 4
D = P * PACK
BATCH = 8
TOKENS = 1024
WINDOW = 4
KEYS = TOKENS // WINDOW
SET = 128
BLOCK = SET * WINDOW
BLOCKS = BATCH * TOKENS // BLOCK
LAST = BLOCKS - 1
BLOCKS_PER_BATCH = TOKENS // BLOCK
PSUM_BANKS = 8
PER_BANK = 2
BANKS = PACK // PER_BANK
HALVES = 2
DIRECT = 1
SCORE_LAG = 2

FLOPS = 2 * BATCH * TOKENS * D * D * 2 + 2 * BATCH * TOKENS * KEYS * D


def tile_siglipsdpaattention_pa_t_kernel(tc, x, Wq, bq, Wk, bk, out):
    nc = tc.nc
    x_rows = x.flatten_outer_dims()
    out_rows = out.flatten_outer_dims()

    with ExitStack() as ctx:
        ctx.enter_context(tc.manual_schedule())

        const = ctx.enter_context(tc.tile_pool(name="const", bufs=1))
        x_pool = ctx.enter_context(tc.tile_pool(name="x_pool", bufs=BLOCKS))
        ordered_pool = ctx.enter_context(tc.tile_pool(name="ordered_pool", bufs=3))
        grouped_pool = ctx.enter_context(tc.tile_pool(name="grouped_pool", bufs=3))
        x_mx_pool = ctx.enter_context(tc.tile_pool(name="x_mx_pool", bufs=3))
        k_mx_pool = ctx.enter_context(tc.tile_pool(name="k_mx_pool", bufs=3))
        q_mx_pool = ctx.enter_context(tc.tile_pool(name="q_mx_pool", bufs=SCORE_LAG + 2))
        out_pool = ctx.enter_context(tc.tile_pool(name="out_pool", bufs=4))
        psum = ctx.enter_context(tc.psum_pool(name="psum", bufs=PSUM_BANKS))

        def mx_operand(pool, columns, label):
            codes = pool.tile([P, columns], U32, name="%s_codes" % label, align_bytes=64)
            scales = pool.tile([P, columns], U8, name="%s_scales" % label, align_bytes=64)
            return codes, scales

        def quantise(grouped, operand, columns):
            codes, scales = operand
            nc.vector.quantize_mx(
                out=codes[:, columns].bitcast(FP8X4), scales=scales[:, columns], in_=grouped
            )

        def mx_pass(acc, stationary, stationary_columns, moving, moving_columns, start=True, stop=True):
            nc.tensor.matmul_mx(
                out=acc,
                lhsT=stationary[0][:, stationary_columns].bitcast(FP8X4),
                lhsT_scale=stationary[1][:, stationary_columns],
                rhs=moving[0][:, moving_columns].bitcast(FP8X4),
                rhs_scale=moving[1][:, moving_columns],
                start=start,
                stop=stop,
            )

        def sets(first, count=1):
            return slice(first * SET, (first + count) * SET)

        def load_rows(rows, rows_sb, pieces=1):
            rows = rows.rearrange("(p s) d -> p s d", s=PACK)
            for piece in range(pieces):
                slots = slice(piece * PACK // pieces, (piece + 1) * PACK // pieces)
                nc.sync.dma_start(out=rows_sb[:, slots, :], in_=rows[:, slots, :])

        def x_block(n):
            return x_rows[n * BLOCK : (n + 1) * BLOCK, :]

        wq_sb = const.tile([P, PACK, D], BF16)
        wk_sb = const.tile([P, PACK, D], BF16)
        x_sb = [x_pool.tile([P, PACK, D], BF16, name="x_sb") for n in range(BLOCKS)]
        load_rows(Wq, wq_sb, pieces=2)
        load_rows(x_block(0), x_sb[0], pieces=2)
        load_rows(Wk, wk_sb)
        for n in range(1, BLOCKS):
            load_rows(x_block(n), x_sb[n])

        bq_bf = const.tile([P, PACK], BF16)
        bk_bf = const.tile([P, PACK], BF16)
        nc.scalar.dma_start(out=bq_bf[:], in_=bq.rearrange("(p j) -> p j", j=PACK))
        nc.scalar.dma_start(out=bk_bf[:], in_=bk.rearrange("(p j) -> p j", j=PACK))

        ident = const.tile([P, P], F32)
        make_identity(nc, ident[:])

        def order_pairs(rows_sb):
            ordered = ordered_pool.tile([P, HALVES, PACK, P], F32, name="ordered")
            nc.vector.tensor_copy(
                out=ordered[:], in_=rows_sb[:].bitcast(F32).rearrange("p s (q u) -> p u s q", u=HALVES)
            )
            return ordered

        def in_order(ordered):
            return lambda s, u: ordered[:, u, s, :]

        def every_second(rows_sb):
            return lambda s, u: rows_sb[:, s, :].bitcast(F32)[:, u::HALVES]

        def bank_to_partitions(pairs, grouped, bank, copy_out):
            grouped_pairs = grouped[:].bitcast(F32).rearrange("p (c u) -> p c u", u=HALVES)
            flipped = psum.tile([P, HALVES, PER_BANK * SET], F32, name="flipped", tag="bank")
            for i in range(PER_BANK):
                for u in range(HALVES):
                    nc.tensor.transpose(flipped[:, u, sets(i)], pairs(PER_BANK * bank + i, u), ident[:])
            copy_out(
                out=grouped_pairs[:, sets(PER_BANK * bank, PER_BANK), :],
                in_=flipped[:].rearrange("p u c -> p c u"),
            )

        zeros = const.tile([P, BLOCK], BF16)
        nc.vector.memset(zeros[:], 0.0)

        def raise_clock(count):
            scrap = psum.tile([P, BLOCK], F32, name="scrap", tag="bank")
            for i in range(count):
                nc.tensor.matmul(scrap[:], lhsT=zeros[:, sets(0)], rhs=zeros[:], start=True, stop=True)

        bq_f32 = const.tile([P, PACK], F32)
        bk_f32 = const.tile([P, PACK], F32)

        wq_grouped = const.tile([P, PACK * D], BF16, align_bytes=64)
        wk_grouped = const.tile([P, PACK * D], BF16, align_bytes=64)
        wq_mx = mx_operand(const, D, "wq")
        wk_mx = mx_operand(const, D, "wk")
        x_pairs = {}
        x_mx = {}

        def new_x_grouped():
            return grouped_pool.tile([P, PACK * BLOCK], BF16, name="x_grouped", align_bytes=64)

        def quantise_x(n, x_grouped):
            x_mx[n] = mx_operand(x_mx_pool, BLOCK, "x")
            quantise(x_grouped[:], x_mx[n], sets(0, WINDOW))

        def order_x(n):
            x_pairs[n] = in_order(order_pairs(x_sb[n]))

        for n in range(DIRECT):
            x_pairs[n] = every_second(x_sb[n])
        raise_clock(3)
        nc.vector.tensor_copy(out=bq_f32[:], in_=bq_bf[:])
        nc.vector.tensor_copy(out=bk_f32[:], in_=bk_bf[:])
        first_x_grouped = new_x_grouped()
        copies = (nc.scalar.copy, nc.vector.tensor_copy)
        for bank in range(BANKS):
            bank_to_partitions(every_second(wq_sb), wq_grouped, bank, copies[bank])
        quantise(wq_grouped[:], wq_mx, sets(0, PACK))
        for bank in range(BANKS):
            bank_to_partitions(x_pairs[0], first_x_grouped, bank, nc.scalar.copy)
        raise_clock(2)
        quantise_x(0, first_x_grouped)
        for bank in range(BANKS):
            bank_to_partitions(every_second(wk_sb), wk_grouped, bank, nc.scalar.copy)
        order_x(1)
        quantise(wk_grouped[:], wk_mx, sets(0, PACK))
        order_x(2)

        bq_every_column = bq_f32[:].unsqueeze(1).to_broadcast([P, SET, PACK])
        bk_every_column = bk_f32[:].unsqueeze(1).to_broadcast([P, SET, PACK])

        q_grouped = {}
        q_mx = {}
        k_grouped = {}
        k_mx = {}

        def prepare_x(n):
            x_grouped = new_x_grouped()
            for bank in range(BANKS):
                bank_to_partitions(x_pairs[n], x_grouped, bank, nc.scalar.copy)
            quantise_x(n, x_grouped)

        def new_q(n):
            q_grouped[n] = grouped_pool.tile([P, BLOCK, PACK], BF16, name="q_grouped", align_bytes=64)
            q_mx[n] = mx_operand(q_mx_pool, BLOCK, "q")

        def copy_on_gpsimd(out, in_):
            nc.gpsimd.tensor_scalar(out=out, in0=in_, scalar1=1.0, scalar2=0.0, op0=MULT, op1=ADD)

        def q_of_sets_2_and_3(n, interleave):
            q_planes = grouped_pool.tile([P, PACK, 2 * SET], BF16, name="q_planes")
            for bank in range(BANKS):
                q_acc = psum.tile([P, PER_BANK, 2 * SET], F32, name="q_acc_planes", tag="bank")
                for i in range(PER_BANK):
                    mx_pass(q_acc[:, i, :], wq_mx, sets(PER_BANK * bank + i), x_mx[n], sets(2, 2))
                for i in range(PER_BANK):
                    j = PER_BANK * bank + i
                    nc.scalar.activation(
                        out=q_planes[:, j, :], in_=q_acc[:, i, :], func=IDENTITY,
                        bias=bq_f32[:, j : j + 1], scale=1.0,
                    )
            interleave(out=q_grouped[n][:, sets(2, 2), :], in_=q_planes[:].rearrange("p j c -> p c j"))

        def q_of_sets_0_and_1(n):
            for r in range(2):
                q_acc = psum.tile([P, PACK, SET], F32, name="q_acc", tag="bank")
                for j in range(PACK):
                    mx_pass(q_acc[:, j, :], wq_mx, sets(j), x_mx[n], sets(r))
                nc.vector.tensor_tensor(
                    out=q_grouped[n][:, sets(r), :], in0=q_acc[:].rearrange("p j c -> p c j"),
                    in1=bq_every_column, op=ADD,
                )

        def quantise_q(n, first=0, count=WINDOW):
            columns = sets(first, count)
            quantise(q_grouped[n][:, columns, :].rearrange("p c j -> p (c j)"), q_mx[n], columns)

        def merged_k(n):
            k_acc = psum.tile([P, PACK, SET], F32, name="k_acc", tag="bank")
            for j in range(PACK):
                for r in range(WINDOW):
                    mx_pass(
                        k_acc[:, j, :], wk_mx, sets(j), x_mx[n], sets(r),
                        start=(r == 0), stop=(r == WINDOW - 1),
                    )
            k_grouped[n] = grouped_pool.tile([P, SET, PACK], BF16, name="k_grouped", align_bytes=64)
            nc.vector.scalar_tensor_tensor(
                out=k_grouped[n][:], in0=k_acc[:].rearrange("p j m -> p m j"), scalar=1.0 / WINDOW,
                in1=bk_every_column, op0=MULT, op1=ADD,
            )

        def quantise_k(n):
            b, part = divmod(n, BLOCKS_PER_BATCH)
            if part == 0:
                k_mx[b] = mx_operand(k_mx_pool, KEYS, "k")
            quantise(k_grouped[n][:].rearrange("p m j -> p (m j)"), k_mx[b], sets(part))

        def scale_on_scalar(out, in_):
            nc.scalar.activation(
                out=out, in_=in_, func=COPY, bias=math.log(WINDOW), scale=1.0 / math.sqrt(D)
            )

        def scale_on_vector(out, in_):
            nc.vector.tensor_scalar(
                out=out, in0=in_, scalar1=1.0 / math.sqrt(D), scalar2=math.log(WINDOW),
                op0=MULT, op1=ADD,
            )

        def scores(n, bank, scale):
            block_rows = out_rows[n * BLOCK : (n + 1) * BLOCK, :].rearrange("(m r) k -> m r k", r=WINDOW)
            first = PER_BANK * bank
            score_acc = psum.tile([P, PER_BANK, KEYS], F32, name="score_acc", tag="bank")
            for i in range(PER_BANK):
                mx_pass(score_acc[:, i, :], q_mx[n], sets(first + i), k_mx[n // BLOCKS_PER_BATCH], sets(0, 2))
            logits = out_pool.tile([P, PER_BANK, KEYS], F32, name="logits")
            scale(out=logits[:], in_=score_acc[:])
            nc.sync.dma_start(out=block_rows[:, first : first + PER_BANK, :], in_=logits[:])

        new_q(0)
        q_of_sets_2_and_3(0, copy_on_gpsimd)
        q_of_sets_0_and_1(0)
        prepare_x(1)
        merged_k(0)
        quantise_k(0)
        order_x(3)
        for n in range(1, LAST):
            prepare_x(n + 1)
            quantise_q(n - 1)
            new_q(n)
            q_of_sets_2_and_3(n, copy_on_gpsimd)
            merged_k(n)
            if n >= SCORE_LAG:
                for bank in range(BANKS):
                    scores(n - SCORE_LAG, bank, scale_on_scalar)
            q_of_sets_0_and_1(n)
            quantise_k(n)
            if n + 3 < BLOCKS:
                order_x(n + 3)

        quantise_q(LAST - 1)
        new_q(LAST)
        q_of_sets_2_and_3(LAST, copy_on_gpsimd)
        merged_k(LAST)
        for bank in range(BANKS):
            scores(LAST - 2, bank, scale_on_scalar)
        quantise_k(LAST)
        q_of_sets_0_and_1(LAST)
        for bank in range(BANKS):
            scores(LAST - 1, bank, scale_on_scalar)
        quantise_q(LAST, 2, 2)
        quantise_q(LAST, 0, 2)
        scores(LAST, 1, scale_on_vector)
        scores(LAST, 0, scale_on_scalar)
